import numpy as np
import ml_dtypes


def mxq(x, axis, fmt="e4m3"):
    dtype, down = {"e4m3": (ml_dtypes.float8_e4m3fn, 7), "e5m2": (ml_dtypes.float8_e5m2, 14)}[fmt]
    v = np.moveaxis(np.asarray(x, np.float32).astype(ml_dtypes.bfloat16).astype(np.float64), axis, -1)
    blocks = v.reshape(v.shape[:-1] + (-1, 32))
    amax = np.abs(blocks).max(-1, keepdims=True)
    byte = np.maximum(np.where(amax > 0, np.frexp(amax)[1] - 1 + 127, 0) - down, 1)
    scale = np.exp2(byte - 127.0)
    codes = (blocks / scale).astype(np.float32).astype(dtype).astype(np.float64)
    return np.moveaxis((codes * scale).reshape(v.shape), -1, axis)


WIDE = False


def mx_kscale(k):
    if not WIDE:
        return np.ones(k)
    levels = np.array([10, -10, 5, -5, 0])
    a = np.random.permutation(np.resize(levels, k // 512 * 4)).reshape(k // 512, 4)
    idx = np.arange(k)
    return np.exp2(a[idx // 512, idx % 128 // 32])


BF16 = ml_dtypes.bfloat16


def bf(x):
    return np.asarray(x, np.float32).astype(BF16)


def f64(x):
    return np.asarray(x).astype(np.float64)


B, C, D, O = 8, 256, 4096, 256
S0 = 1
S = 2
P = D // (S * (S0 + 1))
K = S * C


def setup_inputs():
    s = mx_kscale(K).reshape(S, C)
    sx = np.tile(np.repeat(s.T, S0 + 1, axis=1), (1, P))
    return {"x": bf(np.random.standard_normal((B, C, D)) * sx),
            "weight": bf(np.random.standard_normal((O, C, 1, S)) / C ** 0.25 / s.T[None, :, None, :])}


def reference(x, weight):
    xp = f64(x).reshape(B, C, D // (S0 + 1), S0 + 1).sum(axis=-1)
    xr = xp.reshape(B, C, P, S)
    a = xr.transpose(0, 2, 3, 1).reshape(B, P, K)
    w = f64(weight)[:, :, 0, :].transpose(2, 1, 0).reshape(K, O)
    out = (mxq(a, 2, "e4m3") @ mxq(w, 0, "e4m3")) / np.sqrt(C)
    return out.transpose(0, 2, 1)

@@ -1,0 +1,113 @@
+from contextlib import ExitStack
+
+import concourse.mybir as mybir
+from concourse.masks import make_identity
+
+BF16 = mybir.dt.bfloat16
+F32 = mybir.dt.float32
+U32 = mybir.dt.uint32
+U8 = mybir.dt.uint8
+FP8X4 = mybir.dt.float8_e4m3fn_x4
+ADD = mybir.AluOpType.add
+COPY = mybir.ActivationFunctionType.Copy
+
+B, C, D, O = 8, 256, 4096, 256
+POS = D // 4
+P = 128
+N_TILE = 512
+FLOPS = 2 * B * POS * (2 * C) * O
+
+
+def tile_nonoverlappingconv1d_shared_t_kernel(tc, x, weight, out):
+    nc = tc.nc
+    with ExitStack() as ctx:
+        const = ctx.enter_context(tc.tile_pool(name="const", bufs=1))
+        xpool = ctx.enter_context(tc.tile_pool(name="xpool", bufs=1))
+        opool = ctx.enter_context(tc.tile_pool(name="opool", bufs=1))
+        work = ctx.enter_context(tc.tile_pool(name="work", bufs=3))
+        psum_w = ctx.enter_context(tc.psum_pool(name="psum_w", bufs=1))
+        psum = ctx.enter_context(tc.psum_pool(name="psum", bufs=6))
+        ctx.enter_context(tc.manual_schedule())
+
+        w_sb = const.tile([P, 2 * 2 * C], BF16, name="w_sb")
+        nc.scalar.dma_start(
+            out=w_sb[:].rearrange("q (m f) -> q m f", m=2),
+            in_=weight.rearrange("(q m) c u k -> q m (c u k)", m=2),
+        )
+        chunks = []
+        for b in range(B):
+            xb = x[b].rearrange("(p e) d -> p e d", e=2)
+            parts = 2 if b == 0 else 1
+            width = D // parts
+            for h in range(parts):
+                xt = xpool.tile([P, 2, width], BF16, name="xt%d_%d" % (b, h))
+                nc.sync.dma_start(out=xt[:], in_=xb[:, :, h * width : (h + 1) * width])
+                for j in range(width // (4 * N_TILE)):
+                    chunks.append((xt, j * N_TILE, b, h * (width // 4) + j * N_TILE))
+
+        ident = const.tile([P, P], F32, name="ident")
+        make_identity(nc, ident[:])
+        w_words = w_sb[:].bitcast(F32).rearrange("q (m p u) -> q m u p", m=2, u=2)
+        wt = psum_w.tile([P, 2, 2, P], F32, name="wt")
+        for m in range(2):
+            for u in range(2):
+                nc.tensor.transpose(out=wt[:, m, u, :], in_=w_words[:, m, u, :], identity=ident[:])
+        wg = const.tile([P, 2 * P * 4], BF16, name="wg", align_bytes=64)
+        nc.scalar.copy(
+            out=wg[:].bitcast(F32).rearrange("p (m q u) -> p m q u", m=2, u=2),
+            in_=wt[:].rearrange("p m u q -> p m q u"),
+        )
+        w_codes = const.tile([P, 2 * P], U32, name="w_codes", align_bytes=64)
+        w_scales = const.tile([P, 2 * P], U8, name="w_scales", align_bytes=64)
+
+        grouped = {}
+        quantised = {}
+        out_tiles = {}
+
+        def pair_sum(i):
+            xt, n0, b, nb = chunks[i]
+            g = work.tile([P, 4 * N_TILE], BF16, name="g", align_bytes=64)
+            xv = xt[:].rearrange("p e (n k s) -> p n e k s", k=2, s=2)
+            nc.vector.tensor_tensor(
+                out=g[:].rearrange("p (n e k) -> p n e k", e=2, k=2),
+                in0=xv[:, n0 : n0 + N_TILE, :, :, 0],
+                in1=xv[:, n0 : n0 + N_TILE, :, :, 1],
+                op=ADD,
+            )
+            grouped[i] = g
+
+        def quantise(i):
+            codes = work.tile([P, N_TILE], U32, name="codes", align_bytes=64)
+            scales = work.tile([P, N_TILE], U8, name="scales", align_bytes=64)
+            nc.vector.quantize_mx(out=codes[:].bitcast(FP8X4), scales=scales[:], in_=grouped[i][:])
+            quantised[i] = (codes, scales)
+
+        def multiply(i):
+            xt, n0, b, nb = chunks[i]
+            codes, scales = quantised[i]
+            if nb == 0:
+                out_tiles[b] = opool.tile([P, 2, POS], F32, name="osb%d" % b)
+            osb = out_tiles[b]
+            for m in range(2):
+                ps = psum.tile([P, N_TILE], F32, name="ps")
+                nc.tensor.matmul_mx(
+                    out=ps[:],
+                    lhsT=w_codes[:, m * P : (m + 1) * P].bitcast(FP8X4),
+                    lhsT_scale=w_scales[:, m * P : (m + 1) * P],
+                    rhs=codes[:].bitcast(FP8X4),
+                    rhs_scale=scales[:],
+                    start=True,
+                    stop=True,
+                )
+                nc.scalar.activation(out=osb[:, m, nb : nb + N_TILE], in_=ps[:], func=COPY, scale=1.0 / 16.0)
+            if nb + N_TILE == POS:
+                nc.sync.dma_start(out=out[b].rearrange("(q m) n -> q m n", m=2), in_=osb[:])
+
+        pair_sum(0)
+        nc.vector.quantize_mx(out=w_codes[:].bitcast(FP8X4), scales=w_scales[:], in_=wg[:])
+        for i in range(1, len(chunks)):
+            pair_sum(i)
+            quantise(i - 1)
+            multiply(i - 1)
+        quantise(len(chunks) - 1)
+        multiply(len(chunks) - 1)

@@ -14,8 +14,16 @@ COPY = mybir.ActivationFunctionType.Copy
 B, C, D, O = 8, 256, 4096, 256
 POS = D // 4
 P = 128
-N_TILE = 512
 FLOPS = 2 * B * POS * (2 * C) * O
+
+LOADS = {0: [512, 512], 1: [512, 512]}
+CHUNKS = {}
+PE_POS = {10: 512, 12: 256}
+PE_AFTER = {7: [(10, 0), (10, 1), (10, 2), (10, 3)], 9: [(12, 0), (12, 1)]}
+W_AFTER_LOAD = -1
+QW_AFTER = 0
+LAST_SPLIT = False
+HALF_STORES = []
 
 
 def tile_nonoverlappingconv1d_shared_t_kernel(tc, x, weight, out):
@@ -26,27 +34,48 @@ def tile_nonoverlappingconv1d_shared_t_kernel(tc, x, weight, out):
         opool = ctx.enter_context(tc.tile_pool(name="opool", bufs=1))
         work = ctx.enter_context(tc.tile_pool(name="work", bufs=3))
         psum_w = ctx.enter_context(tc.psum_pool(name="psum_w", bufs=1))
-        psum = ctx.enter_context(tc.psum_pool(name="psum", bufs=6))
+        psum_s = ctx.enter_context(tc.psum_pool(name="psum_s", bufs=2))
+        psum = ctx.enter_context(tc.psum_pool(name="psum", bufs=5))
         ctx.enter_context(tc.manual_schedule())
 
         w_sb = const.tile([P, 2 * 2 * C], BF16, name="w_sb")
-        nc.scalar.dma_start(
-            out=w_sb[:].rearrange("q (m f) -> q m f", m=2),
-            in_=weight.rearrange("(q m) c u k -> q m (c u k)", m=2),
-        )
+
+        def load_w(queue):
+            queue.dma_start(
+                out=w_sb[:].rearrange("q (m f) -> q m f", m=2),
+                in_=weight.rearrange("(q m) c u k -> q m (c u k)", m=2),
+            )
+
+        if W_AFTER_LOAD < 0:
+            load_w(nc.scalar)
         chunks = []
+        n_loads = 0
         for b in range(B):
             xb = x[b].rearrange("(p e) d -> p e d", e=2)
-            parts = 2 if b == 0 else 1
-            width = D // parts
-            for h in range(parts):
-                xt = xpool.tile([P, 2, width], BF16, name="xt%d_%d" % (b, h))
-                nc.sync.dma_start(out=xt[:], in_=xb[:, :, h * width : (h + 1) * width])
-                for j in range(width // (4 * N_TILE)):
-                    chunks.append((xt, j * N_TILE, b, h * (width // 4) + j * N_TILE))
+            loads = LOADS.get(b, [POS])
+            sizes = CHUNKS.get(b, [512, 512])
+            tiles = []
+            start = 0
+            for npos in loads:
+                xt = xpool.tile([P, 2, 4 * npos], BF16, name="xt%d_%d" % (b, start))
+                nc.sync.dma_start(out=xt[:], in_=xb[:, :, 4 * start : 4 * (start + npos)])
+                tiles.append((xt, start, npos))
+                start += npos
+                n_loads += 1
+                if n_loads == W_AFTER_LOAD:
+                    load_w(nc.sync)
+            start = 0
+            for npos in sizes:
+                for xt, t0, tn in tiles:
+                    if t0 <= start and start + npos <= t0 + tn:
+                        chunks.append((xt, start - t0, b, start, npos))
+                start += npos
+        n_chunks = len(chunks)
 
         ident = const.tile([P, P], F32, name="ident")
         make_identity(nc, ident[:])
+        ident_bf = const.tile([P, P], BF16, name="ident_bf")
+        make_identity(nc, ident_bf[:])
         w_words = w_sb[:].bitcast(F32).rearrange("q (m p u) -> q m u p", m=2, u=2)
         wt = psum_w.tile([P, 2, 2, P], F32, name="wt")
         for m in range(2):
@@ -64,34 +93,63 @@ def tile_nonoverlappingconv1d_shared_t_kernel(tc, x, weight, out):
         quantised = {}
         out_tiles = {}
 
+        def group_tile(i):
+            if i not in grouped:
+                npos = chunks[i][4]
+                if i in PE_POS:
+                    grouped[i] = const.tile([P, 4 * npos], BF16, name="g_pe%d" % i, align_bytes=64)
+                else:
+                    g = work.tile([P, 4 * npos], BF16, name="g", align_bytes=64)
+                    grouped[i] = g
+            return grouped[i]
+
         def pair_sum(i):
-            xt, n0, b, nb = chunks[i]
-            g = work.tile([P, 4 * N_TILE], BF16, name="g", align_bytes=64)
+            xt, n0, b, nb, npos = chunks[i]
+            skip = PE_POS.get(i, 0)
+            if skip == npos:
+                return
+            g = group_tile(i)
             xv = xt[:].rearrange("p e (n k s) -> p n e k s", k=2, s=2)
             nc.vector.tensor_tensor(
-                out=g[:].rearrange("p (n e k) -> p n e k", e=2, k=2),
-                in0=xv[:, n0 : n0 + N_TILE, :, :, 0],
-                in1=xv[:, n0 : n0 + N_TILE, :, :, 1],
+                out=g[:, 4 * skip :].rearrange("p (n e k) -> p n e k", e=2, k=2),
+                in0=xv[:, n0 + skip : n0 + npos, :, :, 0],
+                in1=xv[:, n0 + skip : n0 + npos, :, :, 1],
                 op=ADD,
             )
-            grouped[i] = g
+
+        def pe_sum(i, r):
+            xt, n0, b, nb, npos = chunks[i]
+            g = group_tile(i)
+            xv = xt[:].rearrange("p e (j s) -> p e j s", s=2)
+            j0 = 2 * (n0 + P * r)
+            sp = psum_s.tile([P, 2, 2 * P], F32, name="sp")
+            for e in range(2):
+                for s in range(2):
+                    nc.tensor.matmul(
+                        out=sp[:, e, :], lhsT=ident_bf[:], rhs=xv[:, e, j0 : j0 + 2 * P, s], start=(s == 0), stop=(s == 1)
+                    )
+            nc.scalar.copy(
+                out=g[:, 4 * P * r : 4 * P * (r + 1)].rearrange("p (n e k) -> p n e k", e=2, k=2),
+                in_=sp[:].rearrange("p e (n k) -> p n e k", k=2),
+            )
 
         def quantise(i):
-            codes = work.tile([P, N_TILE], U32, name="codes", align_bytes=64)
-            scales = work.tile([P, N_TILE], U8, name="scales", align_bytes=64)
+            npos = chunks[i][4]
+            codes = work.tile([P, npos], U32, name="codes", align_bytes=64)
+            scales = work.tile([P, npos], U8, name="scales", align_bytes=64)
             nc.vector.quantize_mx(out=codes[:].bitcast(FP8X4), scales=scales[:], in_=grouped[i][:])
             quantised[i] = (codes, scales)
 
         def multiply(i):
-            xt, n0, b, nb = chunks[i]
+            xt, n0, b, nb, npos = chunks[i]
             codes, scales = quantised[i]
             if nb == 0:
                 out_tiles[b] = opool.tile([P, 2, POS], F32, name="osb%d" % b)
             osb = out_tiles[b]
             for m in range(2):
-                ps = psum.tile([P, N_TILE], F32, name="ps")
+                ps = psum.tile([P, 512], F32, name="ps")
                 nc.tensor.matmul_mx(
-                    out=ps[:],
+                    out=ps[:, :npos],
                     lhsT=w_codes[:, m * P : (m + 1) * P].bitcast(FP8X4),
                     lhsT_scale=w_scales[:, m * P : (m + 1) * P],
                     rhs=codes[:].bitcast(FP8X4),
@@ -99,15 +157,23 @@ def tile_nonoverlappingconv1d_shared_t_kernel(tc, x, weight, out):
                     start=True,
                     stop=True,
                 )
-                nc.scalar.activation(out=osb[:, m, nb : nb + N_TILE], in_=ps[:], func=COPY, scale=1.0 / 16.0)
-            if nb + N_TILE == POS:
-                nc.sync.dma_start(out=out[b].rearrange("(q m) n -> q m n", m=2), in_=osb[:])
+                if LAST_SPLIT and i == n_chunks - 1 and m == 1:
+                    nc.vector.tensor_scalar_mul(osb[:, m, nb : nb + npos], ps[:, :npos], 1.0 / 16.0)
+                else:
+                    nc.scalar.activation(out=osb[:, m, nb : nb + npos], in_=ps[:, :npos], func=COPY, scale=1.0 / 16.0)
+            ob = out[b].rearrange("(q m) n -> q m n", m=2)
+            if b in HALF_STORES:
+                nc.sync.dma_start(out=ob[:, :, nb : nb + npos], in_=osb[:, :, nb : nb + npos])
+            elif nb + npos == POS:
+                nc.sync.dma_start(out=ob, in_=osb[:])
 
-        pair_sum(0)
-        nc.vector.quantize_mx(out=w_codes[:].bitcast(FP8X4), scales=w_scales[:], in_=wg[:])
-        for i in range(1, len(chunks)):
-            pair_sum(i)
-            quantise(i - 1)
-            multiply(i - 1)
-        quantise(len(chunks) - 1)
-        multiply(len(chunks) - 1)
+        for i in range(n_chunks + 1):
+            if i < n_chunks:
+                pair_sum(i)
+            if i == QW_AFTER:
+                nc.vector.quantize_mx(out=w_codes[:].bitcast(FP8X4), scales=w_scales[:], in_=wg[:])
+            if i >= 1:
+                quantise(i - 1)
+                multiply(i - 1)
+                for ci, r in PE_AFTER.get(i - 1, []):
+                    pe_sum(ci, r)

@@ -16,13 +16,13 @@ POS = D // 4
 P = 128
 FLOPS = 2 * B * POS * (2 * C) * O
 
-LOADS = {0: [512, 512], 1: [512, 512]}
-CHUNKS = {}
+LOADS = {}
+CHUNKS = {7: [512, 256, 256]}
 PE_POS = {10: 512, 12: 256}
 PE_AFTER = {7: [(10, 0), (10, 1), (10, 2), (10, 3)], 9: [(12, 0), (12, 1)]}
-W_AFTER_LOAD = -1
-QW_AFTER = 0
-LAST_SPLIT = False
+W_AFTER_LOAD = 1
+QW_AFTER = 1
+LAST_SPLIT = True
 HALF_STORES = []
 
 

@@ -18,8 +18,8 @@ FLOPS = 2 * B * POS * (2 * C) * O
 
 LOADS = {}
 CHUNKS = {7: [512, 256, 256]}
-PE_POS = {10: 512, 12: 256}
-PE_AFTER = {7: [(10, 0), (10, 1), (10, 2), (10, 3)], 9: [(12, 0), (12, 1)]}
+PE_POS = {}
+PE_AFTER = {}
 W_AFTER_LOAD = 1
 QW_AFTER = 1
 LAST_SPLIT = True
@@ -34,8 +34,7 @@ def tile_nonoverlappingconv1d_shared_t_kernel(tc, x, weight, out):
         opool = ctx.enter_context(tc.tile_pool(name="opool", bufs=1))
         work = ctx.enter_context(tc.tile_pool(name="work", bufs=3))
         psum_w = ctx.enter_context(tc.psum_pool(name="psum_w", bufs=1))
-        psum_s = ctx.enter_context(tc.psum_pool(name="psum_s", bufs=2))
-        psum = ctx.enter_context(tc.psum_pool(name="psum", bufs=5))
+        psum = ctx.enter_context(tc.psum_pool(name="psum", bufs=6))
         ctx.enter_context(tc.manual_schedule())
 
         w_sb = const.tile([P, 2 * 2 * C], BF16, name="w_sb")
@@ -74,8 +73,6 @@ def tile_nonoverlappingconv1d_shared_t_kernel(tc, x, weight, out):
 
         ident = const.tile([P, P], F32, name="ident")
         make_identity(nc, ident[:])
-        ident_bf = const.tile([P, P], BF16, name="ident_bf")
-        make_identity(nc, ident_bf[:])
         w_words = w_sb[:].bitcast(F32).rearrange("q (m p u) -> q m u p", m=2, u=2)
         wt = psum_w.tile([P, 2, 2, P], F32, name="wt")
         for m in range(2):
@@ -115,22 +112,6 @@ def tile_nonoverlappingconv1d_shared_t_kernel(tc, x, weight, out):
                 in0=xv[:, n0 + skip : n0 + npos, :, :, 0],
                 in1=xv[:, n0 + skip : n0 + npos, :, :, 1],
                 op=ADD,
-            )
-
-        def pe_sum(i, r):
-            xt, n0, b, nb, npos = chunks[i]
-            g = group_tile(i)
-            xv = xt[:].rearrange("p e (j s) -> p e j s", s=2)
-            j0 = 2 * (n0 + P * r)
-            sp = psum_s.tile([P, 2, 2 * P], F32, name="sp")
-            for e in range(2):
-                for s in range(2):
-                    nc.tensor.matmul(
-                        out=sp[:, e, :], lhsT=ident_bf[:], rhs=xv[:, e, j0 : j0 + 2 * P, s], start=(s == 0), stop=(s == 1)
-                    )
-            nc.scalar.copy(
-                out=g[:, 4 * P * r : 4 * P * (r + 1)].rearrange("p (n e k) -> p n e k", e=2, k=2),
-                in_=sp[:].rearrange("p e (n k) -> p n e k", k=2),
             )
 
         def quantise(i):
@@ -175,5 +156,3 @@ def tile_nonoverlappingconv1d_shared_t_kernel(tc, x, weight, out):
             if i >= 1:
                 quantise(i - 1)
                 multiply(i - 1)
-                for ci, r in PE_AFTER.get(i - 1, []):
-                    pe_sum(ci, r)

from contextlib import ExitStack

import concourse.mybir as mybir
from concourse.masks import make_identity

BF16 = mybir.dt.bfloat16
F32 = mybir.dt.float32
U32 = mybir.dt.uint32
U8 = mybir.dt.uint8
FP8X4 = mybir.dt.float8_e4m3fn_x4
ADD = mybir.AluOpType.add
COPY = mybir.ActivationFunctionType.Copy

B, C, D, O = 8, 256, 4096, 256
POS = D // 4
P = 128
FLOPS = 2 * B * POS * (2 * C) * O

LOADS = {}
CHUNKS = {7: [512, 256, 256]}
PE_POS = {}
PE_AFTER = {}
W_AFTER_LOAD = 1
QW_AFTER = 1
LAST_SPLIT = True
HALF_STORES = []


def tile_nonoverlappingconv1d_shared_t_kernel(tc, x, weight, out):
    nc = tc.nc
    with ExitStack() as ctx:
        const = ctx.enter_context(tc.tile_pool(name="const", bufs=1))
        xpool = ctx.enter_context(tc.tile_pool(name="xpool", bufs=1))
        opool = ctx.enter_context(tc.tile_pool(name="opool", bufs=1))
        work = ctx.enter_context(tc.tile_pool(name="work", bufs=3))
        psum_w = ctx.enter_context(tc.psum_pool(name="psum_w", bufs=1))
        psum = ctx.enter_context(tc.psum_pool(name="psum", bufs=6))
        ctx.enter_context(tc.manual_schedule())

        w_sb = const.tile([P, 2 * 2 * C], BF16, name="w_sb")

        def load_w(queue):
            queue.dma_start(
                out=w_sb[:].rearrange("q (m f) -> q m f", m=2),
                in_=weight.rearrange("(q m) c u k -> q m (c u k)", m=2),
            )

        if W_AFTER_LOAD < 0:
            load_w(nc.scalar)
        chunks = []
        n_loads = 0
        for b in range(B):
            xb = x[b].rearrange("(p e) d -> p e d", e=2)
            loads = LOADS.get(b, [POS])
            sizes = CHUNKS.get(b, [512, 512])
            tiles = []
            start = 0
            for npos in loads:
                xt = xpool.tile([P, 2, 4 * npos], BF16, name="xt%d_%d" % (b, start))
                nc.sync.dma_start(out=xt[:], in_=xb[:, :, 4 * start : 4 * (start + npos)])
                tiles.append((xt, start, npos))
                start += npos
                n_loads += 1
                if n_loads == W_AFTER_LOAD:
                    load_w(nc.sync)
            start = 0
            for npos in sizes:
                for xt, t0, tn in tiles:
                    if t0 <= start and start + npos <= t0 + tn:
                        chunks.append((xt, start - t0, b, start, npos))
                start += npos
        n_chunks = len(chunks)

        ident = const.tile([P, P], F32, name="ident")
        make_identity(nc, ident[:])
        w_words = w_sb[:].bitcast(F32).rearrange("q (m p u) -> q m u p", m=2, u=2)
        wt = psum_w.tile([P, 2, 2, P], F32, name="wt")
        for m in range(2):
            for u in range(2):
                nc.tensor.transpose(out=wt[:, m, u, :], in_=w_words[:, m, u, :], identity=ident[:])
        wg = const.tile([P, 2 * P * 4], BF16, name="wg", align_bytes=64)
        nc.scalar.copy(
            out=wg[:].bitcast(F32).rearrange("p (m q u) -> p m q u", m=2, u=2),
            in_=wt[:].rearrange("p m u q -> p m q u"),
        )
        w_codes = const.tile([P, 2 * P], U32, name="w_codes", align_bytes=64)
        w_scales = const.tile([P, 2 * P], U8, name="w_scales", align_bytes=64)

        grouped = {}
        quantised = {}
        out_tiles = {}

        def group_tile(i):
            if i not in grouped:
                npos = chunks[i][4]
                if i in PE_POS:
                    grouped[i] = const.tile([P, 4 * npos], BF16, name="g_pe%d" % i, align_bytes=64)
                else:
                    g = work.tile([P, 4 * npos], BF16, name="g", align_bytes=64)
                    grouped[i] = g
            return grouped[i]

        def pair_sum(i):
            xt, n0, b, nb, npos = chunks[i]
            skip = PE_POS.get(i, 0)
            if skip == npos:
                return
            g = group_tile(i)
            xv = xt[:].rearrange("p e (n k s) -> p n e k s", k=2, s=2)
            nc.vector.tensor_tensor(
                out=g[:, 4 * skip :].rearrange("p (n e k) -> p n e k", e=2, k=2),
                in0=xv[:, n0 + skip : n0 + npos, :, :, 0],
                in1=xv[:, n0 + skip : n0 + npos, :, :, 1],
                op=ADD,
            )

        def quantise(i):
            npos = chunks[i][4]
            codes = work.tile([P, npos], U32, name="codes", align_bytes=64)
            scales = work.tile([P, npos], U8, name="scales", align_bytes=64)
            nc.vector.quantize_mx(out=codes[:].bitcast(FP8X4), scales=scales[:], in_=grouped[i][:])
            quantised[i] = (codes, scales)

        def multiply(i):
            xt, n0, b, nb, npos = chunks[i]
            codes, scales = quantised[i]
            if nb == 0:
                out_tiles[b] = opool.tile([P, 2, POS], F32, name="osb%d" % b)
            osb = out_tiles[b]
            for m in range(2):
                ps = psum.tile([P, 512], F32, name="ps")
                nc.tensor.matmul_mx(
                    out=ps[:, :npos],
                    lhsT=w_codes[:, m * P : (m + 1) * P].bitcast(FP8X4),
                    lhsT_scale=w_scales[:, m * P : (m + 1) * P],
                    rhs=codes[:].bitcast(FP8X4),
                    rhs_scale=scales[:],
                    start=True,
                    stop=True,
                )
                if LAST_SPLIT and i == n_chunks - 1 and m == 1:
                    nc.vector.tensor_scalar_mul(osb[:, m, nb : nb + npos], ps[:, :npos], 1.0 / 16.0)
                else:
                    nc.scalar.activation(out=osb[:, m, nb : nb + npos], in_=ps[:, :npos], func=COPY, scale=1.0 / 16.0)
            ob = out[b].rearrange("(q m) n -> q m n", m=2)
            if b in HALF_STORES:
                nc.sync.dma_start(out=ob[:, :, nb : nb + npos], in_=osb[:, :, nb : nb + npos])
            elif nb + npos == POS:
                nc.sync.dma_start(out=ob, in_=osb[:])

        for i in range(n_chunks + 1):
            if i < n_chunks:
                pair_sum(i)
            if i == QW_AFTER:
                nc.vector.quantize_mx(out=w_codes[:].bitcast(FP8X4), scales=w_scales[:], in_=wg[:])
            if i >= 1:
                quantise(i - 1)
                multiply(i - 1)
